import numpy as np
import ml_dtypes


def mxq(x, axis, fmt="e4m3"):
    dtype, down = {"e4m3": (ml_dtypes.float8_e4m3fn, 7), "e5m2": (ml_dtypes.float8_e5m2, 14)}[fmt]
    v = np.moveaxis(np.asarray(x, np.float32).astype(ml_dtypes.bfloat16).astype(np.float64), axis, -1)
    blocks = v.reshape(v.shape[:-1] + (-1, 32))
    amax = np.abs(blocks).max(-1, keepdims=True)
    byte = np.maximum(np.where(amax > 0, np.frexp(amax)[1] - 1 + 127, 0) - down, 1)
    scale = np.exp2(byte - 127.0)
    codes = (blocks / scale).astype(np.float32).astype(dtype).astype(np.float64)
    return np.moveaxis((codes * scale).reshape(v.shape), -1, axis)


WIDE = False


def mx_kscale(k):
    if not WIDE:
        return np.ones(k)
    levels = np.array([10, -10, 5, -5, 0])
    a = np.random.permutation(np.resize(levels, k // 512 * 4)).reshape(k // 512, 4)
    idx = np.arange(k)
    return np.exp2(a[idx // 512, idx % 128 // 32])


BF16 = ml_dtypes.bfloat16


def bf(x):
    return np.asarray(x, np.float32).astype(BF16)


def f64(x):
    return np.asarray(x).astype(np.float64)


N, DIN, DI, DH, DO, G = 1024, 1024, 1024, 1024, 1024, 16
DH2 = 2 * DH
EPS = 1e-5


def erf(v):
    a = np.minimum(np.abs(v), 6.0)
    term = a.copy()
    tot = a.copy()
    for n in range(1, 120):
        term = term * (2.0 * a * a / (2 * n + 1))
        tot = tot + term
    return np.sign(v) * (2.0 / np.sqrt(np.pi)) * np.exp(-a * a) * tot


def gelu_erf(v):
    return 0.5 * v * (1.0 + erf(v / np.sqrt(2.0)))


def setup_inputs():
    s, u = mx_kscale(DI), mx_kscale(DO)
    tt = np.array(mx_kscale(DH2), dtype=np.float64)
    tt[:DH] = 1.0
    t = tt[DH:]
    return {"h_ret": bf(np.random.standard_normal((N, DI)) * 0.6 * s),
            "h_prime": bf(np.random.standard_normal((N, DO)) * u),
            "Wr": bf(np.random.standard_normal((DH, DI)) * 2.0 / np.sqrt(DI) / s[None, :]),
            "br": bf(np.random.standard_normal(DH) * 0.2),
            "Wc": bf(np.random.standard_normal((DH, DO)) / np.sqrt(DO) * t[:, None] / u[None, :]),
            "bc": bf(np.random.standard_normal(DH) * 0.2 * t),
            "Wp": bf(np.random.standard_normal((DO, DH2)) / np.sqrt(DH2) / tt[None, :]),
            "bp": bf(np.random.standard_normal(DO) * 0.2),
            "prelu_w": bf(0.25 + 0.1 * np.random.standard_normal(DO)),
            "gn_w": bf(1.0 + 0.1 * np.random.standard_normal(DO)),
            "gn_b": bf(0.1 * np.random.standard_normal(DO))}


def reference(h_ret, h_prime, Wr, br, Wc, bc, Wp, bp, prelu_w, gn_w, gn_b):
    a = gelu_erf((mxq(f64(h_ret), 1, "e4m3") @ mxq(f64(Wr), 1, "e4m3").T) + f64(br))
    c = (mxq(f64(h_prime), 1, "e4m3") @ mxq(f64(Wc), 1, "e4m3").T) + f64(bc)
    combined = np.concatenate([a, c], axis=-1)
    x = (mxq(combined, 1, "e4m3") @ mxq(f64(Wp), 1, "e4m3").T) + f64(bp)
    x = np.where(x >= 0, x, f64(prelu_w)[None, :] * x)
    xg = x.T.reshape(G, -1)
    mean = xg.mean(axis=1, keepdims=True)
    var = xg.var(axis=1, keepdims=True)
    xg = (xg - mean) / np.sqrt(var + EPS)
    xt = xg.reshape(DO, N) * f64(gn_w)[:, None] + f64(gn_b)[:, None]
    return np.ascontiguousarray(xt.T)

@@ -1,0 +1,309 @@
+from contextlib import ExitStack
+
+import concourse.masks as masks
+import concourse.mybir as mybir
+
+F32 = mybir.dt.float32
+BF16 = mybir.dt.bfloat16
+U32 = mybir.dt.uint32
+U8 = mybir.dt.uint8
+FP8X4 = mybir.dt.float8_e4m3fn_x4
+ACT = mybir.ActivationFunctionType
+ALU = mybir.AluOpType
+
+P = 128
+ROWS = 1024
+CHANNELS = 1024
+HALF = 512
+CHUNK = 4096
+CHUNK_WORDS = CHUNK // 4
+N_CHUNKS = 12
+N_QUADS = 8
+N_TILES = 8
+LEAD = 3
+RAW_BUFS = 6
+GROUP_SIZE = 64 * ROWS
+EPS = 1e-5
+
+FLOPS = 2 * ROWS * 1024 * 1024 * 2 + 2 * ROWS * 2048 * CHANNELS
+
+
+def tile_parallelretention_pb_kernel(
+    tc, h_ret, h_prime, Wr, br, Wc, bc, Wp, bp, prelu_w, gn_w, gn_b, out
+):
+    nc = tc.nc
+    with ExitStack() as ctx:
+        ctx.enter_context(tc.manual_schedule())
+        const = ctx.enter_context(tc.tile_pool(name="const", bufs=1))
+        raw_pool = ctx.enter_context(tc.tile_pool(name="raw", bufs=RAW_BUFS))
+        grouped_pool = ctx.enter_context(tc.tile_pool(name="grouped", bufs=3))
+        stage1 = ctx.enter_context(tc.tile_pool(name="stage1", bufs=2))
+        stage2 = ctx.enter_context(tc.tile_pool(name="stage2", bufs=3))
+        small = ctx.enter_context(tc.tile_pool(name="small", bufs=4))
+        psum = ctx.enter_context(tc.psum_pool(name="psum", bufs=4))
+
+        def tokens(h, half):
+            return h.rearrange("(p r) k -> p r k", r=8)[:, 4 * half : 4 * half + 4, :]
+
+        def hidden(w, jj):
+            return w.rearrange("(j p e) k -> p j (e k)", p=P, e=2)[:, 2 * jj : 2 * jj + 2, :]
+
+        def channels(mm):
+            return Wp.rearrange("(m p) k -> p m k", p=P)[:, 2 * mm : 2 * mm + 2, :]
+
+        chunk_src = [
+            tokens(h_ret, 0), hidden(Wr, 0), tokens(h_ret, 1), hidden(Wr, 1),
+            tokens(h_prime, 0), hidden(Wc, 0), tokens(h_prime, 1), hidden(Wc, 1),
+            channels(0), channels(1), channels(2), channels(3),
+        ]
+        raws = {}
+        groupeds = {}
+
+        def load_chunk(i):
+            raw = raw_pool.tile([P, CHUNK], BF16)
+            src = chunk_src[i]
+            nc.sync.dma_start(
+                out=raw[:].rearrange("p (a x) -> p a x", a=src.shape[1]), in_=src
+            )
+            raws[i] = raw
+
+        rows16 = const.tile([32, P], BF16)
+        for v, vec in enumerate((bp, prelu_w, gn_w, gn_b)):
+            nc.scalar.dma_start(
+                out=rows16[8 * v : 8 * v + 8, :], in_=vec.rearrange("(m i) -> m i", i=P)
+            )
+        rows32 = const.tile([P, P], F32)
+        nc.vector.memset(rows32[:], 0.0)
+        nc.scalar.dma_start(
+            out=rows32[32:36, :], in_=br.rearrange("(r w) -> r w", w=2 * P).bitcast(F32)
+        )
+        nc.scalar.dma_start(
+            out=rows32[36:40, :], in_=bc.rearrange("(r w) -> r w", w=2 * P).bitcast(F32)
+        )
+        for i in range(RAW_BUFS):
+            load_chunk(i)
+
+        warm = const.tile([P, 1], F32)
+        nc.vector.memset(warm[:], 0.0)
+        nc.scalar.activation(out=warm[:], in_=warm[:], func=ACT.Gelu)
+
+        ident = const.tile([P, P], F32)
+        masks.make_identity(nc, ident[:])
+        group_mean = const.tile([P, P], F32)
+        nc.vector.memset(group_mean[:], 0.0)
+        nc.vector.memset(group_mean[0:64, 0:64], 1.0 / GROUP_SIZE)
+        nc.vector.memset(group_mean[64:128, 64:128], 1.0 / GROUP_SIZE)
+        neg_half = const.tile([P, 1], F32)
+        nc.vector.memset(neg_half[:], -0.5)
+        sums = const.tile([P, N_TILES, 16], F32)
+        nc.vector.memset(sums[:], 0.0)
+
+        nc.vector.tensor_copy(out=rows32[0:32, :], in_=rows16[:])
+        turned = psum.tile([P, 4, P], F32, tag="tp")
+        nc.tensor.transpose(turned[:, 0, :], rows32[:], ident[:])
+        chan = const.tile([P, 32], F32)
+        nc.vector.tensor_copy(out=chan[:], in_=turned[:, 0, 0:32])
+        bias_words = const.tile([P, 8], F32)
+        nc.vector.tensor_copy(out=bias_words[:], in_=turned[:, 0, 32:40])
+        bias1 = const.tile([P, 16], F32)
+        nc.vector.tensor_copy(out=bias1[:], in_=bias_words[:].bitcast(BF16))
+        neg_bp = const.tile([P, N_TILES], F32)
+        nc.vector.tensor_scalar_mul(out=neg_bp[:], in0=chan[:, 0:8], scalar1=-1.0)
+        one_minus_w = const.tile([P, N_TILES], F32)
+        nc.vector.tensor_scalar(
+            out=one_minus_w[:], in0=chan[:, 8:16], scalar1=-1.0, scalar2=1.0,
+            op0=ALU.mult, op1=ALU.add,
+        )
+        nc.vector.tensor_scalar_mul(out=sums[:, :, 2], in0=chan[:, 0:8], scalar1=float(ROWS))
+
+        codes_in = const.tile([P, N_CHUNKS, CHUNK_WORDS], U32, align_bytes=64)
+        scales_in = const.tile([P, N_CHUNKS, CHUNK_WORDS], U8, align_bytes=64)
+        codes_ac = const.tile([P, N_QUADS, HALF], U32, align_bytes=64)
+        scales_ac = const.tile([P, N_QUADS, HALF], U8, align_bytes=64)
+
+        def transpose_chunk(i):
+            words = raws[i][:].bitcast(F32).rearrange("p (b w) -> p b w", b=4)
+            grouped = grouped_pool.tile([P, CHUNK], BF16, align_bytes=64)
+            grouped_words = grouped[:].bitcast(F32).rearrange("p (g c u) -> p g c u", g=2, u=2)
+            for g in range(2):
+                for pair in range(2):
+                    bank = psum.tile([P, 2, 2 * P], F32, tag="tp")
+                    for u in range(2):
+                        for s in range(2):
+                            nc.tensor.transpose(
+                                bank[:, u, P * s : P * (s + 1)],
+                                words[:, 2 * pair + s, 256 * g + P * u : 256 * g + P * (u + 1)],
+                                ident[:],
+                            )
+                    dst = grouped_words[:, g, 2 * P * pair : 2 * P * (pair + 1), :]
+                    src = bank[:].rearrange("p u c -> p c u")
+                    if g == 0 and pair == 0:
+                        nc.vector.tensor_copy(out=dst, in_=src)
+                    else:
+                        nc.scalar.copy(out=dst, in_=src)
+            groupeds[i] = grouped
+
+        def quantise_chunk(i):
+            nc.vector.quantize_mx(
+                out=codes_in[:, i, :].bitcast(FP8X4), scales=scales_in[:, i, :], in_=groupeds[i][:]
+            )
+
+        planes_of = {}
+        regrouped_of = {}
+
+        def stage1_matmuls(k):
+            s, jj, half = k // 4, (k // 2) % 2, k % 2
+            h_chunk, w_chunk = 4 * s + 2 * half, 4 * s + 2 * jj + 1
+            planes = stage1.tile([P, 4, HALF], BF16)
+            for t in range(4):
+                acc = psum.tile([P, HALF], F32, tag="mx")
+                for g in range(2):
+                    w_cols = slice(HALF * g + P * t, HALF * g + P * (t + 1))
+                    h_cols = slice(HALF * g, HALF * (g + 1))
+                    nc.tensor.matmul_mx(
+                        out=acc[:],
+                        lhsT=codes_in[:, w_chunk, w_cols].bitcast(FP8X4),
+                        lhsT_scale=scales_in[:, w_chunk, w_cols],
+                        rhs=codes_in[:, h_chunk, h_cols].bitcast(FP8X4),
+                        rhs_scale=scales_in[:, h_chunk, h_cols],
+                        start=(g == 0),
+                        stop=(g == 1),
+                    )
+                col = 8 * s + 4 * jj + t
+                nc.scalar.activation(
+                    out=planes[:, t, :], in_=acc[:], func=(ACT.Gelu if s == 0 else ACT.Identity),
+                    bias=bias1[:, col : col + 1], scale=1.0,
+                )
+            planes_of[k] = planes
+
+        def regroup(k):
+            regrouped = stage1.tile([P, HALF, 4], BF16, align_bytes=64)
+            nc.vector.tensor_copy(
+                out=regrouped[:].rearrange("p (c i) t -> p c t i", i=4),
+                in_=planes_of[k][:].rearrange("p t (c i) -> p c t i", i=4),
+            )
+            regrouped_of[k] = regrouped
+
+        def quantise_unit(k):
+            nc.vector.quantize_mx(
+                out=codes_ac[:, k, :].bitcast(FP8X4), scales=scales_ac[:, k, :],
+                in_=regrouped_of[k][:].rearrange("p n t -> p (n t)"),
+            )
+
+        shifted_of = {}
+        norm_of = {}
+        normed_of = {}
+
+        def stage2_matmuls(m):
+            w_chunk, m2 = 8 + m // 2, m % 2
+            shifted = stage2.tile([P, ROWS], F32, bufs=4)
+            for half in range(2):
+                acc = psum.tile([P, HALF], F32, tag="mx")
+                for g in range(4):
+                    w0 = HALF * (g % 2) + P * (2 * m2 + g // 2)
+                    nc.tensor.matmul_mx(
+                        out=acc[:],
+                        lhsT=codes_in[:, w_chunk, w0 : w0 + P].bitcast(FP8X4),
+                        lhsT_scale=scales_in[:, w_chunk, w0 : w0 + P],
+                        rhs=codes_ac[:, 2 * g + half, :].bitcast(FP8X4),
+                        rhs_scale=scales_ac[:, 2 * g + half, :],
+                        start=(g == 0),
+                        stop=(g == 3),
+                    )
+                neg_part = stage2.tile([P, HALF], F32)
+                nc.scalar.activation(
+                    out=neg_part[:], in_=acc[:], func=ACT.Relu, bias=neg_bp[:, m : m + 1], scale=-1.0
+                )
+                nc.vector.scalar_tensor_tensor(
+                    out=shifted[:, HALF * half : HALF * (half + 1)], in0=neg_part[:],
+                    scalar=one_minus_w[:, m : m + 1], in1=acc[:], op0=ALU.mult, op1=ALU.add,
+                    accum_out=sums[:, m, half : half + 1],
+                )
+            for half in range(2):
+                squares = stage2.tile([P, HALF], BF16)
+                nc.scalar.activation(
+                    out=squares[:], in_=shifted[:, HALF * half : HALF * (half + 1)], func=ACT.Square,
+                    bias=chan[:, m : m + 1], scale=1.0, accum_out=sums[:, m, 8 + half : 9 + half],
+                )
+            shifted_of[m] = shifted
+
+        def statistics(m):
+            spread = psum.tile([P, 4, P], F32, tag="tp")
+            nc.tensor.matmul(
+                out=spread[:, 0, 0:16], lhsT=group_mean[:], rhs=sums[:, m, :], start=True, stop=True
+            )
+            moments = small.tile([P, 2], F32)
+            nc.vector.tensor_reduce(
+                out=moments[:], in_=spread[:, 0, 0:16].rearrange("p (b c) -> p b c", b=2),
+                axis=mybir.AxisListType.X, op=ALU.add,
+            )
+            norm = small.tile([P, 8], F32)
+            mean = moments[:, 0:1]
+            nc.gpsimd.tensor_tensor(out=norm[:, 0:1], in0=mean, in1=mean, op=ALU.mult)
+            nc.gpsimd.tensor_scalar(
+                out=norm[:, 1:2], in0=moments[:, 1:2], scalar1=norm[:, 0:1], scalar2=EPS,
+                op0=ALU.subtract, op1=ALU.add,
+            )
+            nc.gpsimd.tensor_tensor(out=norm[:, 2:3], in0=norm[:, 1:2], in1=neg_half[:], op=ALU.pow)
+            nc.gpsimd.tensor_tensor(
+                out=norm[:, 3:4], in0=norm[:, 2:3], in1=chan[:, 16 + m : 17 + m], op=ALU.mult
+            )
+            nc.gpsimd.tensor_tensor(
+                out=norm[:, 4:5], in0=chan[:, m : m + 1], in1=mean, op=ALU.subtract
+            )
+            nc.gpsimd.tensor_scalar(
+                out=norm[:, 5:6], in0=norm[:, 4:5], scalar1=norm[:, 3:4],
+                scalar2=chan[:, 24 + m : 25 + m], op0=ALU.mult, op1=ALU.add,
+            )
+            norm_of[m] = norm
+
+        def normalise(m):
+            normed = stage2.tile([P, ROWS], F32)
+            nc.vector.tensor_scalar(
+                out=normed[:], in0=shifted_of[m][:], scalar1=norm_of[m][:, 3:4],
+                scalar2=norm_of[m][:, 5:6], op0=ALU.mult, op1=ALU.add,
+            )
+            normed_of[m] = normed
+
+        def store_tile(m):
+            staged = stage2.tile([P, 8, P], F32)
+            for half in range(2):
+                bank = psum.tile([P, 4, P], F32, tag="tp")
+                for r in range(4):
+                    c0 = HALF * half + P * r
+                    nc.tensor.transpose(bank[:, r, :], normed_of[m][:, c0 : c0 + P], ident[:])
+                if half == 0:
+                    nc.scalar.copy(out=staged[:, 0:4, :], in_=bank[:])
+                else:
+                    nc.vector.tensor_copy(out=staged[:, 4:8, :], in_=bank[:])
+            nc.sync.dma_start(
+                out=out.rearrange("(p r) c -> p r c", r=8)[:, :, P * m : P * (m + 1)], in_=staged[:]
+            )
+
+        transpose_chunk(0)
+        transpose_chunk(1)
+        quantise_chunk(0)
+        transpose_chunk(2)
+        quantise_chunk(1)
+        quantise_chunk(2)
+        for k in range(N_QUADS):
+            i = k + LEAD
+            stage1_matmuls(k)
+            transpose_chunk(i)
+            if k + RAW_BUFS < N_CHUNKS:
+                load_chunk(k + RAW_BUFS)
+            regroup(k)
+            quantise_chunk(i)
+            quantise_unit(k)
+        transpose_chunk(N_CHUNKS - 1)
+        quantise_chunk(N_CHUNKS - 1)
+
+        for step in range(N_TILES + 3):
+            if step < N_TILES:
+                stage2_matmuls(step)
+            if 0 <= step - 1 < N_TILES:
+                statistics(step - 1)
+            if 0 <= step - 3 < N_TILES:
+                store_tile(step - 3)
+            if 0 <= step - 2 < N_TILES:
+                normalise(step - 2)

@@ -98,23 +98,29 @@ def tile_parallelretention_pb_kernel(
         sums = const.tile([P, N_TILES, 16], F32)
         nc.vector.memset(sums[:], 0.0)
 
-        nc.vector.tensor_copy(out=rows32[0:32, :], in_=rows16[:])
-        turned = psum.tile([P, 4, P], F32, tag="tp")
-        nc.tensor.transpose(turned[:, 0, :], rows32[:], ident[:])
         chan = const.tile([P, 32], F32)
-        nc.vector.tensor_copy(out=chan[:], in_=turned[:, 0, 0:32])
         bias_words = const.tile([P, 8], F32)
-        nc.vector.tensor_copy(out=bias_words[:], in_=turned[:, 0, 32:40])
         bias1 = const.tile([P, 16], F32)
-        nc.vector.tensor_copy(out=bias1[:], in_=bias_words[:].bitcast(BF16))
         neg_bp = const.tile([P, N_TILES], F32)
-        nc.vector.tensor_scalar_mul(out=neg_bp[:], in0=chan[:, 0:8], scalar1=-1.0)
         one_minus_w = const.tile([P, N_TILES], F32)
-        nc.vector.tensor_scalar(
-            out=one_minus_w[:], in0=chan[:, 8:16], scalar1=-1.0, scalar2=1.0,
-            op0=ALU.mult, op1=ALU.add,
-        )
-        nc.vector.tensor_scalar_mul(out=sums[:, :, 2], in0=chan[:, 0:8], scalar1=float(ROWS))
+        turned_of = {}
+
+        def turn_vectors():
+            turned = psum.tile([P, 4, P], F32, tag="tp")
+            nc.tensor.transpose(turned[:, 0, :], rows32[:], ident[:])
+            turned_of[0] = turned
+
+        def spread_vectors():
+            turned = turned_of[0]
+            nc.vector.tensor_copy(out=bias_words[:], in_=turned[:, 0, 32:40])
+            nc.vector.tensor_copy(out=chan[:], in_=turned[:, 0, 0:32])
+            nc.vector.tensor_copy(out=bias1[:], in_=bias_words[:].bitcast(BF16))
+            nc.vector.tensor_scalar_mul(out=neg_bp[:], in0=chan[:, 0:8], scalar1=-1.0)
+            nc.vector.tensor_scalar(
+                out=one_minus_w[:], in0=chan[:, 8:16], scalar1=-1.0, scalar2=1.0,
+                op0=ALU.mult, op1=ALU.add,
+            )
+            nc.vector.tensor_scalar_mul(out=sums[:, :, 2], in0=chan[:, 0:8], scalar1=float(ROWS))
 
         codes_in = const.tile([P, N_CHUNKS, CHUNK_WORDS], U32, align_bytes=64)
         scales_in = const.tile([P, N_CHUNKS, CHUNK_WORDS], U8, align_bytes=64)
@@ -283,8 +289,11 @@ def tile_parallelretention_pb_kernel(
         transpose_chunk(0)
         transpose_chunk(1)
         quantise_chunk(0)
+        nc.vector.tensor_copy(out=rows32[0:32, :], in_=rows16[:])
         transpose_chunk(2)
+        turn_vectors()
         quantise_chunk(1)
+        spread_vectors()
         quantise_chunk(2)
         for k in range(N_QUADS):
             i = k + LEAD
@@ -303,7 +312,7 @@ def tile_parallelretention_pb_kernel(
                 stage2_matmuls(step)
             if 0 <= step - 1 < N_TILES:
                 statistics(step - 1)
-            if 0 <= step - 3 < N_TILES:
-                store_tile(step - 3)
             if 0 <= step - 2 < N_TILES:
                 normalise(step - 2)
+            if 0 <= step - 3 < N_TILES:
+                store_tile(step - 3)

@@ -11,6 +11,7 @@ FP8X4 = mybir.dt.float8_e4m3fn_x4
 ACT = mybir.ActivationFunctionType
 ALU = mybir.AluOpType
 
+BETWEEN = 1
 P = 128
 ROWS = 1024
 CHANNELS = 1024
@@ -18,12 +19,14 @@ HALF = 512
 CHUNK = 4096
 CHUNK_WORDS = CHUNK // 4
 N_CHUNKS = 12
-N_QUADS = 8
+N_UNITS = 8
 N_TILES = 8
-LEAD = 3
 RAW_BUFS = 6
 GROUP_SIZE = 64 * ROWS
 EPS = 1e-5
+CHUNK_ORDER = (0, 1, 4, 5, 2, 6, 3, 7, 8, 9, 10, 11)
+UNIT_ORDER = (0, 4, 1, 5, 2, 6, 3, 7)
+LEAD = 4
 
 FLOPS = 2 * ROWS * 1024 * 1024 * 2 + 2 * ROWS * 2048 * CHANNELS
 
@@ -80,7 +83,7 @@ def tile_parallelretention_pb_kernel(
         nc.scalar.dma_start(
             out=rows32[36:40, :], in_=bc.rearrange("(r w) -> r w", w=2 * P).bitcast(F32)
         )
-        for i in range(RAW_BUFS):
+        for i in CHUNK_ORDER[:RAW_BUFS]:
             load_chunk(i)
 
         warm = const.tile([P, 1], F32)
@@ -124,10 +127,10 @@ def tile_parallelretention_pb_kernel(
 
         codes_in = const.tile([P, N_CHUNKS, CHUNK_WORDS], U32, align_bytes=64)
         scales_in = const.tile([P, N_CHUNKS, CHUNK_WORDS], U8, align_bytes=64)
-        codes_ac = const.tile([P, N_QUADS, HALF], U32, align_bytes=64)
-        scales_ac = const.tile([P, N_QUADS, HALF], U8, align_bytes=64)
+        codes_ac = const.tile([P, N_UNITS, HALF], U32, align_bytes=64)
+        scales_ac = const.tile([P, N_UNITS, HALF], U8, align_bytes=64)
 
-        def transpose_chunk(i):
+        def transpose_chunk(i, vector_banks):
             words = raws[i][:].bitcast(F32).rearrange("p (b w) -> p b w", b=4)
             grouped = grouped_pool.tile([P, CHUNK], BF16, align_bytes=64)
             grouped_words = grouped[:].bitcast(F32).rearrange("p (g c u) -> p g c u", g=2, u=2)
@@ -143,7 +146,7 @@ def tile_parallelretention_pb_kernel(
                             )
                     dst = grouped_words[:, g, 2 * P * pair : 2 * P * (pair + 1), :]
                     src = bank[:].rearrange("p u c -> p c u")
-                    if g == 0 and pair == 0:
+                    if 2 * g + pair in vector_banks:
                         nc.vector.tensor_copy(out=dst, in_=src)
                     else:
                         nc.scalar.copy(out=dst, in_=src)
@@ -157,9 +160,12 @@ def tile_parallelretention_pb_kernel(
         planes_of = {}
         regrouped_of = {}
 
-        def stage1_matmuls(k):
+        def operands(k):
             s, jj, half = k // 4, (k // 2) % 2, k % 2
-            h_chunk, w_chunk = 4 * s + 2 * half, 4 * s + 2 * jj + 1
+            return 4 * s + 2 * half, 4 * s + 2 * jj + 1, 8 * s + 4 * jj
+
+        def stage1_gelu(k):
+            h_chunk, w_chunk, col = operands(k)
             planes = stage1.tile([P, 4, HALF], BF16)
             for t in range(4):
                 acc = psum.tile([P, HALF], F32, tag="mx")
@@ -175,10 +181,9 @@ def tile_parallelretention_pb_kernel(
                         start=(g == 0),
                         stop=(g == 1),
                     )
-                col = 8 * s + 4 * jj + t
                 nc.scalar.activation(
-                    out=planes[:, t, :], in_=acc[:], func=(ACT.Gelu if s == 0 else ACT.Identity),
-                    bias=bias1[:, col : col + 1], scale=1.0,
+                    out=planes[:, t, :], in_=acc[:], func=ACT.Gelu,
+                    bias=bias1[:, col + t : col + t + 1], scale=1.0,
                 )
             planes_of[k] = planes
 
@@ -188,6 +193,34 @@ def tile_parallelretention_pb_kernel(
                 out=regrouped[:].rearrange("p (c i) t -> p c t i", i=4),
                 in_=planes_of[k][:].rearrange("p t (c i) -> p c t i", i=4),
             )
+            regrouped_of[k] = regrouped
+
+        def stage1_linear(k, chunk_between):
+            h_chunk, w_chunk, col = operands(k)
+            regrouped = stage1.tile([P, HALF, 4], BF16, align_bytes=64)
+            for b in range(4):
+                if b == BETWEEN:
+                    quantise_chunk(chunk_between)
+                acc = psum.tile([P, 4, P], F32, tag="mx")
+                for t in range(4):
+                    for g in range(2):
+                        w_cols = slice(HALF * g + P * t, HALF * g + P * (t + 1))
+                        h_cols = slice(HALF * g + P * b, HALF * g + P * (b + 1))
+                        nc.tensor.matmul_mx(
+                            out=acc[:, t, :],
+                            lhsT=codes_in[:, w_chunk, w_cols].bitcast(FP8X4),
+                            lhsT_scale=scales_in[:, w_chunk, w_cols],
+                            rhs=codes_in[:, h_chunk, h_cols].bitcast(FP8X4),
+                            rhs_scale=scales_in[:, h_chunk, h_cols],
+                            start=(g == 0),
+                            stop=(g == 1),
+                        )
+                nc.vector.tensor_tensor(
+                    out=regrouped[:, P * b : P * (b + 1), :],
+                    in0=acc[:].rearrange("p t n -> p n t"),
+                    in1=bias1[:, col : col + 4].unsqueeze(1).to_broadcast([P, P, 4]),
+                    op=ALU.add,
+                )
             regrouped_of[k] = regrouped
 
         def quantise_unit(k):
@@ -286,26 +319,34 @@ def tile_parallelretention_pb_kernel(
                 out=out.rearrange("(p r) c -> p r c", r=8)[:, :, P * m : P * (m + 1)], in_=staged[:]
             )
 
-        transpose_chunk(0)
-        transpose_chunk(1)
+
+        transpose_chunk(0, (0, 2))
+        transpose_chunk(1, (0, 2))
         quantise_chunk(0)
         nc.vector.tensor_copy(out=rows32[0:32, :], in_=rows16[:])
-        transpose_chunk(2)
+        transpose_chunk(4, (0, 2))
         turn_vectors()
         quantise_chunk(1)
         spread_vectors()
-        quantise_chunk(2)
-        for k in range(N_QUADS):
-            i = k + LEAD
-            stage1_matmuls(k)
-            transpose_chunk(i)
-            if k + RAW_BUFS < N_CHUNKS:
-                load_chunk(k + RAW_BUFS)
-            regroup(k)
-            quantise_chunk(i)
-            quantise_unit(k)
-        transpose_chunk(N_CHUNKS - 1)
-        quantise_chunk(N_CHUNKS - 1)
+        transpose_chunk(5, (0, 2))
+        quantise_chunk(4)
+        for j, k in enumerate(UNIT_ORDER):
+            before = CHUNK_ORDER[j + LEAD - 1]
+            if j > 0:
+                quantise_unit(UNIT_ORDER[j - 1])
+            if k < 4:
+                quantise_chunk(before)
+                stage1_gelu(k)
+            else:
+                stage1_linear(k, before)
+            transpose_chunk(CHUNK_ORDER[j + LEAD], ())
+            if j + RAW_BUFS < N_CHUNKS:
+                load_chunk(CHUNK_ORDER[j + RAW_BUFS])
+            if k < 4:
+                regroup(k)
+        quantise_unit(UNIT_ORDER[-1])
+
+        quantise_chunk(CHUNK_ORDER[-1])
 
         for step in range(N_TILES + 3):
             if step < N_TILES:

@@ -12,6 +12,7 @@ ACT = mybir.ActivationFunctionType
 ALU = mybir.AluOpType
 
 BETWEEN = 1
+HALVED = 2
 P = 128
 ROWS = 1024
 CHANNELS = 1024
@@ -62,12 +63,17 @@ def tile_parallelretention_pb_kernel(
         raws = {}
         groupeds = {}
 
-        def load_chunk(i):
+        def load_chunk(i, in_halves=False):
             raw = raw_pool.tile([P, CHUNK], BF16)
             src = chunk_src[i]
-            nc.sync.dma_start(
-                out=raw[:].rearrange("p (a x) -> p a x", a=src.shape[1]), in_=src
-            )
+            rows = src.shape[1]
+            view = raw[:].rearrange("p (a x) -> p a x", a=rows)
+            if in_halves:
+                for pair in range(2):
+                    part = slice(rows // 2 * pair, rows // 2 * (pair + 1))
+                    nc.sync.dma_start(out=view[:, part, :], in_=src[:, part, :])
+            else:
+                nc.sync.dma_start(out=view, in_=src)
             raws[i] = raw
 
         rows16 = const.tile([32, P], BF16)
@@ -83,8 +89,8 @@ def tile_parallelretention_pb_kernel(
         nc.scalar.dma_start(
             out=rows32[36:40, :], in_=bc.rearrange("(r w) -> r w", w=2 * P).bitcast(F32)
         )
-        for i in CHUNK_ORDER[:RAW_BUFS]:
-            load_chunk(i)
+        for n, i in enumerate(CHUNK_ORDER[:RAW_BUFS]):
+            load_chunk(i, in_halves=(n < HALVED))
 
         warm = const.tile([P, 1], F32)
         nc.vector.memset(warm[:], 0.0)
@@ -134,8 +140,8 @@ def tile_parallelretention_pb_kernel(
             words = raws[i][:].bitcast(F32).rearrange("p (b w) -> p b w", b=4)
             grouped = grouped_pool.tile([P, CHUNK], BF16, align_bytes=64)
             grouped_words = grouped[:].bitcast(F32).rearrange("p (g c u) -> p g c u", g=2, u=2)
-            for g in range(2):
-                for pair in range(2):
+            for pair in range(2):
+                for g in range(2):
                     bank = psum.tile([P, 2, 2 * P], F32, tag="tp")
                     for u in range(2):
                         for s in range(2):
@@ -146,7 +152,7 @@ def tile_parallelretention_pb_kernel(
                             )
                     dst = grouped_words[:, g, 2 * P * pair : 2 * P * (pair + 1), :]
                     src = bank[:].rearrange("p u c -> p c u")
-                    if 2 * g + pair in vector_banks:
+                    if 2 * pair + g in vector_banks:
                         nc.vector.tensor_copy(out=dst, in_=src)
                     else:
                         nc.scalar.copy(out=dst, in_=src)
@@ -249,6 +255,8 @@ def tile_parallelretention_pb_kernel(
                         start=(g == 0),
                         stop=(g == 3),
                     )
+                if half == 1 and m > 0:
+                    statistics(m - 1)
                 neg_part = stage2.tile([P, HALF], F32)
                 nc.scalar.activation(
                     out=neg_part[:], in_=acc[:], func=ACT.Relu, bias=neg_bp[:, m : m + 1], scale=-1.0
@@ -298,14 +306,19 @@ def tile_parallelretention_pb_kernel(
 
         def normalise(m):
             normed = stage2.tile([P, ROWS], F32)
-            nc.vector.tensor_scalar(
-                out=normed[:], in0=shifted_of[m][:], scalar1=norm_of[m][:, 3:4],
-                scalar2=norm_of[m][:, 5:6], op0=ALU.mult, op1=ALU.add,
-            )
+            pieces = 2 if m == N_TILES - 1 else 1
+            width = ROWS // pieces
+            for c in range(pieces):
+                nc.vector.tensor_scalar(
+                    out=normed[:, width * c : width * (c + 1)],
+                    in0=shifted_of[m][:, width * c : width * (c + 1)], scalar1=norm_of[m][:, 3:4],
+                    scalar2=norm_of[m][:, 5:6], op0=ALU.mult, op1=ALU.add,
+                )
             normed_of[m] = normed
 
         def store_tile(m):
-            staged = stage2.tile([P, 8, P], F32)
+            staged = stage2.tile([P, 8, P], F32, bufs=4)
+            dst = out.rearrange("(p r) c -> p r c", r=8)[:, :, P * m : P * (m + 1)]
             for half in range(2):
                 bank = psum.tile([P, 4, P], F32, tag="tp")
                 for r in range(4):
@@ -315,9 +328,12 @@ def tile_parallelretention_pb_kernel(
                     nc.scalar.copy(out=staged[:, 0:4, :], in_=bank[:])
                 else:
                     nc.vector.tensor_copy(out=staged[:, 4:8, :], in_=bank[:])
-            nc.sync.dma_start(
-                out=out.rearrange("(p r) c -> p r c", r=8)[:, :, P * m : P * (m + 1)], in_=staged[:]
-            )
+                if m == N_TILES - 1:
+                    nc.sync.dma_start(
+                        out=dst[:, 4 * half : 4 * half + 4, :], in_=staged[:, 4 * half : 4 * half + 4, :]
+                    )
+            if m < N_TILES - 1:
+                nc.sync.dma_start(out=dst, in_=staged[:])
 
 
         transpose_chunk(0, (0, 2))
@@ -351,7 +367,7 @@ def tile_parallelretention_pb_kernel(
         for step in range(N_TILES + 3):
             if step < N_TILES:
                 stage2_matmuls(step)
-            if 0 <= step - 1 < N_TILES:
+            if step == N_TILES:
                 statistics(step - 1)
             if 0 <= step - 2 < N_TILES:
                 normalise(step - 2)

@@ -12,6 +12,7 @@ ACT = mybir.ActivationFunctionType
 ALU = mybir.AluOpType
 
 BETWEEN = 1
+LAST_PIECES = 2
 HALVED = 2
 P = 128
 ROWS = 1024
@@ -129,7 +130,7 @@ def tile_parallelretention_pb_kernel(
                 out=one_minus_w[:], in0=chan[:, 8:16], scalar1=-1.0, scalar2=1.0,
                 op0=ALU.mult, op1=ALU.add,
             )
-            nc.vector.tensor_scalar_mul(out=sums[:, :, 2], in0=chan[:, 0:8], scalar1=float(ROWS))
+            nc.vector.tensor_scalar_mul(out=sums[:, :, 7], in0=chan[:, 0:8], scalar1=float(ROWS))
 
         codes_in = const.tile([P, N_CHUNKS, CHUNK_WORDS], U32, align_bytes=64)
         scales_in = const.tile([P, N_CHUNKS, CHUNK_WORDS], U8, align_bytes=64)
@@ -236,43 +237,59 @@ def tile_parallelretention_pb_kernel(
             )
 
         shifted_of = {}
+        acc_of = {}
+        staged_of = {}
         norm_of = {}
         normed_of = {}
 
-        def stage2_matmuls(m):
+        def pieces_of(m):
+            return LAST_PIECES if m == N_TILES - 1 else 2
+
+        def stage2_piece(m, j):
             w_chunk, m2 = 8 + m // 2, m % 2
-            shifted = stage2.tile([P, ROWS], F32, bufs=4)
-            for half in range(2):
-                acc = psum.tile([P, HALF], F32, tag="mx")
-                for g in range(4):
-                    w0 = HALF * (g % 2) + P * (2 * m2 + g // 2)
-                    nc.tensor.matmul_mx(
-                        out=acc[:],
-                        lhsT=codes_in[:, w_chunk, w0 : w0 + P].bitcast(FP8X4),
-                        lhsT_scale=scales_in[:, w_chunk, w0 : w0 + P],
-                        rhs=codes_ac[:, 2 * g + half, :].bitcast(FP8X4),
-                        rhs_scale=scales_ac[:, 2 * g + half, :],
-                        start=(g == 0),
-                        stop=(g == 3),
-                    )
-                if half == 1 and m > 0:
-                    statistics(m - 1)
-                neg_part = stage2.tile([P, HALF], F32)
-                nc.scalar.activation(
-                    out=neg_part[:], in_=acc[:], func=ACT.Relu, bias=neg_bp[:, m : m + 1], scale=-1.0
+            width = ROWS // pieces_of(m)
+            half, inside = (width * j) // HALF, (width * j) % HALF
+            if j == 0:
+                shifted = stage2.tile([P, ROWS], F32, bufs=N_TILES)
+                shifted_of[m] = shifted
+            acc = psum.tile([P, HALF], F32, tag="mx")
+            for g in range(4):
+                w0 = HALF * (g % 2) + P * (2 * m2 + g // 2)
+                nc.tensor.matmul_mx(
+                    out=acc[:, 0:width],
+                    lhsT=codes_in[:, w_chunk, w0 : w0 + P].bitcast(FP8X4),
+                    lhsT_scale=scales_in[:, w_chunk, w0 : w0 + P],
+                    rhs=codes_ac[:, 2 * g + half, inside : inside + width].bitcast(FP8X4),
+                    rhs_scale=scales_ac[:, 2 * g + half, inside : inside + width],
+                    start=(g == 0),
+                    stop=(g == 3),
                 )
-                nc.vector.scalar_tensor_tensor(
-                    out=shifted[:, HALF * half : HALF * (half + 1)], in0=neg_part[:],
-                    scalar=one_minus_w[:, m : m + 1], in1=acc[:], op0=ALU.mult, op1=ALU.add,
-                    accum_out=sums[:, m, half : half + 1],
-                )
-            for half in range(2):
-                squares = stage2.tile([P, HALF], BF16)
-                nc.scalar.activation(
-                    out=squares[:], in_=shifted[:, HALF * half : HALF * (half + 1)], func=ACT.Square,
-                    bias=chan[:, m : m + 1], scale=1.0, accum_out=sums[:, m, 8 + half : 9 + half],
-                )
-            shifted_of[m] = shifted
+            acc_of[(m, j)] = acc
+
+        def prelu_piece(m, j):
+            width = ROWS // pieces_of(m)
+            acc = acc_of[(m, j)]
+            neg_part = stage2.tile([P, HALF], F32)
+            nc.scalar.activation(
+                out=neg_part[:, 0:width], in_=acc[:, 0:width], func=ACT.Relu, bias=neg_bp[:, m : m + 1], scale=-1.0
+            )
+            nc.vector.scalar_tensor_tensor(
+                out=shifted_of[m][:, width * j : width * (j + 1)], in0=neg_part[:, 0:width],
+                scalar=one_minus_w[:, m : m + 1], in1=acc[:, 0:width], op0=ALU.mult, op1=ALU.add,
+                accum_out=sums[:, m, j : j + 1],
+            )
+
+        def square_piece(m, j):
+            width = ROWS // pieces_of(m)
+            squares = stage2.tile([P, HALF], BF16)
+            nc.scalar.activation(
+                out=squares[:, 0:width], in_=shifted_of[m][:, width * j : width * (j + 1)], func=ACT.Square,
+                bias=chan[:, m : m + 1], scale=1.0, accum_out=sums[:, m, 8 + j : 9 + j],
+            )
+
+        def square_sums(m):
+            for j in range(pieces_of(m)):
+                square_piece(m, j)
 
         def statistics(m):
             spread = psum.tile([P, 4, P], F32, tag="tp")
@@ -304,37 +321,48 @@ def tile_parallelretention_pb_kernel(
             )
             norm_of[m] = norm
 
-        def normalise(m):
-            normed = stage2.tile([P, ROWS], F32)
-            pieces = 2 if m == N_TILES - 1 else 1
+        def normalise_piece(m, j, pieces):
             width = ROWS // pieces
-            for c in range(pieces):
-                nc.vector.tensor_scalar(
-                    out=normed[:, width * c : width * (c + 1)],
-                    in0=shifted_of[m][:, width * c : width * (c + 1)], scalar1=norm_of[m][:, 3:4],
-                    scalar2=norm_of[m][:, 5:6], op0=ALU.mult, op1=ALU.add,
-                )
-            normed_of[m] = normed
+            part = shifted_of[m][:, width * j : width * (j + 1)]
+            nc.vector.tensor_scalar(
+                out=part, in0=part, scalar1=norm_of[m][:, 3:4], scalar2=norm_of[m][:, 5:6],
+                op0=ALU.mult, op1=ALU.add,
+            )
+
+        def normalise(m):
+            normalise_piece(m, 0, 1)
+
+        def turn_back(m, j, pieces, engine):
+            if j == 0:
+                staged = stage2.tile([P, 8, P], F32, bufs=4)
+                staged_of[m] = staged
+            staged = staged_of[m]
+            n = 8 // pieces
+            bank = psum.tile([P, 4, P], F32, tag="tp")
+            for r in range(n):
+                c0 = P * (n * j + r)
+                nc.tensor.transpose(bank[:, r, :], shifted_of[m][:, c0 : c0 + P], ident[:])
+            if engine == "scalar":
+                nc.scalar.copy(out=staged[:, n * j : n * (j + 1), :], in_=bank[:, 0:n, :])
+            else:
+                nc.vector.tensor_copy(out=staged[:, n * j : n * (j + 1), :], in_=bank[:, 0:n, :])
+
+        def store(m, rows):
+            dst = out.rearrange("(p r) c -> p r c", r=8)[:, :, P * m : P * (m + 1)]
+            nc.sync.dma_start(out=dst[:, rows, :], in_=staged_of[m][:, rows, :])
 
         def store_tile(m):
-            staged = stage2.tile([P, 8, P], F32, bufs=4)
-            dst = out.rearrange("(p r) c -> p r c", r=8)[:, :, P * m : P * (m + 1)]
             for half in range(2):
-                bank = psum.tile([P, 4, P], F32, tag="tp")
-                for r in range(4):
-                    c0 = HALF * half + P * r
-                    nc.tensor.transpose(bank[:, r, :], normed_of[m][:, c0 : c0 + P], ident[:])
-                if half == 0:
-                    nc.scalar.copy(out=staged[:, 0:4, :], in_=bank[:])
-                else:
-                    nc.vector.tensor_copy(out=staged[:, 4:8, :], in_=bank[:])
-                if m == N_TILES - 1:
-                    nc.sync.dma_start(
-                        out=dst[:, 4 * half : 4 * half + 4, :], in_=staged[:, 4 * half : 4 * half + 4, :]
-                    )
-            if m < N_TILES - 1:
-                nc.sync.dma_start(out=dst, in_=staged[:])
+                turn_back(m, half, 2, "scalar" if half == 0 else "vector")
+            store(m, slice(0, 8))
 
+        def finish_last(m, pieces):
+            n = 8 // pieces
+            for j in range(pieces):
+                normalise_piece(m, j, pieces)
+            for j in range(pieces):
+                turn_back(m, j, pieces, "scalar" if j % 2 == 0 else "vector")
+                store(m, slice(n * j, n * (j + 1)))
 
         transpose_chunk(0, (0, 2))
         transpose_chunk(1, (0, 2))
@@ -364,12 +392,24 @@ def tile_parallelretention_pb_kernel(
 
         quantise_chunk(CHUNK_ORDER[-1])
 
-        for step in range(N_TILES + 3):
-            if step < N_TILES:
-                stage2_matmuls(step)
-            if step == N_TILES:
-                statistics(step - 1)
-            if 0 <= step - 2 < N_TILES:
+        for step in range(N_TILES):
+            for j in range(pieces_of(step)):
+                stage2_piece(step, j)
+                if j == pieces_of(step) - 1 and step > 0:
+                    statistics(step - 1)
+                prelu_piece(step, j)
+            if step == N_TILES - 1:
+                square_sums(step)
+            if step >= 2:
                 normalise(step - 2)
-            if 0 <= step - 3 < N_TILES:
+            if step in (4, 6):
+                store_tile(step - 4)
                 store_tile(step - 3)
+            if step < N_TILES - 1:
+                square_sums(step)
+        store_tile(4)
+        statistics(7)
+        normalise(6)
+        store_tile(5)
+        store_tile(6)
+        finish_last(7, 4)

@@ -238,6 +238,7 @@ def tile_parallelretention_pb_kernel(
 
         shifted_of = {}
         acc_of = {}
+        wide_of = {}
         staged_of = {}
         norm_of = {}
         normed_of = {}
@@ -334,7 +335,7 @@ def tile_parallelretention_pb_kernel(
 
         def turn_back(m, j, pieces, engine):
             if j == 0:
-                staged = stage2.tile([P, 8, P], F32, bufs=4)
+                staged = stage2.tile([P, 8, P], F32, bufs=2)
                 staged_of[m] = staged
             staged = staged_of[m]
             n = 8 // pieces
@@ -355,6 +356,28 @@ def tile_parallelretention_pb_kernel(
             for half in range(2):
                 turn_back(m, half, 2, "scalar" if half == 0 else "vector")
             store(m, slice(0, 8))
+
+        def pair_tile(q, t):
+            if t == 0:
+                wide_of[q] = [
+                    stage2.tile([P, 4, 2 * P], F32, name="wide%d" % half, bufs=2) for half in range(2)
+                ]
+            m = 2 * q + t
+            for half in range(2):
+                bank = psum.tile([P, 4, P], F32, tag="tp")
+                for r in range(4):
+                    c0 = HALF * half + P * r
+                    nc.tensor.transpose(bank[:, r, :], shifted_of[m][:, c0 : c0 + P], ident[:])
+                dst = wide_of[q][half][:, :, P * t : P * (t + 1)]
+                if half == 0:
+                    nc.scalar.copy(out=dst, in_=bank[:])
+                else:
+                    nc.vector.tensor_copy(out=dst, in_=bank[:])
+
+        def pair_store(q):
+            dst = out.rearrange("(p r) c -> p r c", r=8)[:, :, 2 * P * q : 2 * P * (q + 1)]
+            for half in range(2):
+                nc.sync.dma_start(out=dst[:, 4 * half : 4 * half + 4, :], in_=wide_of[q][half][:])
 
         def finish_last(m, pieces):
             n = 8 // pieces
@@ -403,13 +426,15 @@ def tile_parallelretention_pb_kernel(
             if step >= 2:
                 normalise(step - 2)
             if step in (4, 6):
-                store_tile(step - 4)
-                store_tile(step - 3)
+                pair_tile(step // 2 - 2, 0)
+                pair_tile(step // 2 - 2, 1)
+                pair_store(step // 2 - 2)
             if step < N_TILES - 1:
                 square_sums(step)
-        store_tile(4)
+        pair_tile(2, 0)
         statistics(7)
         normalise(6)
-        store_tile(5)
+        pair_tile(2, 1)
+        pair_store(2)
         store_tile(6)
         finish_last(7, 4)

@@ -202,11 +202,13 @@ def tile_parallelretention_pb_kernel(
             )
             regrouped_of[k] = regrouped
 
-        def stage1_linear(k, chunk_between):
+        def stage1_linear(k, unit_between, chunk_between):
             h_chunk, w_chunk, col = operands(k)
             regrouped = stage1.tile([P, HALF, 4], BF16, align_bytes=64)
             for b in range(4):
-                if b == BETWEEN:
+                if b == 1:
+                    quantise_unit(unit_between)
+                if b == 2:
                     quantise_chunk(chunk_between)
                 acc = psum.tile([P, 4, P], F32, tag="mx")
                 for t in range(4):
@@ -391,21 +393,21 @@ def tile_parallelretention_pb_kernel(
         transpose_chunk(1, (0, 2))
         quantise_chunk(0)
         nc.vector.tensor_copy(out=rows32[0:32, :], in_=rows16[:])
-        transpose_chunk(4, (0, 2))
+        transpose_chunk(4, ())
         turn_vectors()
         quantise_chunk(1)
         spread_vectors()
-        transpose_chunk(5, (0, 2))
+        transpose_chunk(5, ())
         quantise_chunk(4)
         for j, k in enumerate(UNIT_ORDER):
             before = CHUNK_ORDER[j + LEAD - 1]
-            if j > 0:
-                quantise_unit(UNIT_ORDER[j - 1])
             if k < 4:
                 quantise_chunk(before)
+                if j > 0:
+                    quantise_unit(UNIT_ORDER[j - 1])
                 stage1_gelu(k)
             else:
-                stage1_linear(k, before)
+                stage1_linear(k, UNIT_ORDER[j - 1], before)
             transpose_chunk(CHUNK_ORDER[j + LEAD], ())
             if j + RAW_BUFS < N_CHUNKS:
                 load_chunk(CHUNK_ORDER[j + RAW_BUFS])

@@ -12,6 +12,8 @@ ACT = mybir.ActivationFunctionType
 ALU = mybir.AluOpType
 
 BETWEEN = 1
+FIRST_LATE = 9
+LATE_STEPS = (0, 1, 2)
 LAST_PIECES = 2
 HALVED = 2
 P = 128
@@ -208,7 +210,7 @@ def tile_parallelretention_pb_kernel(
             for b in range(4):
                 if b == 1:
                     quantise_unit(unit_between)
-                if b == 2:
+                if b == 2 and chunk_between is not None:
                     quantise_chunk(chunk_between)
                 acc = psum.tile([P, 4, P], F32, tag="mx")
                 for t in range(4):
@@ -400,9 +402,10 @@ def tile_parallelretention_pb_kernel(
         transpose_chunk(5, ())
         quantise_chunk(4)
         for j, k in enumerate(UNIT_ORDER):
-            before = CHUNK_ORDER[j + LEAD - 1]
+            before = CHUNK_ORDER[j + LEAD - 1] if j + LEAD - 1 < FIRST_LATE else None
             if k < 4:
-                quantise_chunk(before)
+                if before is not None:
+                    quantise_chunk(before)
                 if j > 0:
                     quantise_unit(UNIT_ORDER[j - 1])
                 stage1_gelu(k)
@@ -415,14 +418,14 @@ def tile_parallelretention_pb_kernel(
                 regroup(k)
         quantise_unit(UNIT_ORDER[-1])
 
-        quantise_chunk(CHUNK_ORDER[-1])
-
         for step in range(N_TILES):
             for j in range(pieces_of(step)):
                 stage2_piece(step, j)
                 if j == pieces_of(step) - 1 and step > 0:
                     statistics(step - 1)
                 prelu_piece(step, j)
+            if step in LATE_STEPS:
+                quantise_chunk(FIRST_LATE + LATE_STEPS.index(step))
             if step == N_TILES - 1:
                 square_sums(step)
             if step >= 2:

@@ -12,8 +12,8 @@ ACT = mybir.ActivationFunctionType
 ALU = mybir.AluOpType
 
 BETWEEN = 1
-FIRST_LATE = 9
-LATE_STEPS = (0, 1, 2)
+FIRST_LATE = 10
+LATE_STEPS = (0, 1)
 LAST_PIECES = 2
 HALVED = 2
 P = 128

from contextlib import ExitStack

import concourse.masks as masks
import concourse.mybir as mybir

F32 = mybir.dt.float32
BF16 = mybir.dt.bfloat16
U32 = mybir.dt.uint32
U8 = mybir.dt.uint8
FP8X4 = mybir.dt.float8_e4m3fn_x4
ACT = mybir.ActivationFunctionType
ALU = mybir.AluOpType

BETWEEN = 1
FIRST_LATE = 10
LATE_STEPS = (0, 1)
LAST_PIECES = 2
HALVED = 2
P = 128
ROWS = 1024
CHANNELS = 1024
HALF = 512
CHUNK = 4096
CHUNK_WORDS = CHUNK // 4
N_CHUNKS = 12
N_UNITS = 8
N_TILES = 8
RAW_BUFS = 6
GROUP_SIZE = 64 * ROWS
EPS = 1e-5
CHUNK_ORDER = (0, 1, 4, 5, 2, 6, 3, 7, 8, 9, 10, 11)
UNIT_ORDER = (0, 4, 1, 5, 2, 6, 3, 7)
LEAD = 4

FLOPS = 2 * ROWS * 1024 * 1024 * 2 + 2 * ROWS * 2048 * CHANNELS


def tile_parallelretention_pb_kernel(
    tc, h_ret, h_prime, Wr, br, Wc, bc, Wp, bp, prelu_w, gn_w, gn_b, out
):
    nc = tc.nc
    with ExitStack() as ctx:
        ctx.enter_context(tc.manual_schedule())
        const = ctx.enter_context(tc.tile_pool(name="const", bufs=1))
        raw_pool = ctx.enter_context(tc.tile_pool(name="raw", bufs=RAW_BUFS))
        grouped_pool = ctx.enter_context(tc.tile_pool(name="grouped", bufs=3))
        stage1 = ctx.enter_context(tc.tile_pool(name="stage1", bufs=2))
        stage2 = ctx.enter_context(tc.tile_pool(name="stage2", bufs=3))
        small = ctx.enter_context(tc.tile_pool(name="small", bufs=4))
        psum = ctx.enter_context(tc.psum_pool(name="psum", bufs=4))

        def tokens(h, half):
            return h.rearrange("(p r) k -> p r k", r=8)[:, 4 * half : 4 * half + 4, :]

        def hidden(w, jj):
            return w.rearrange("(j p e) k -> p j (e k)", p=P, e=2)[:, 2 * jj : 2 * jj + 2, :]

        def channels(mm):
            return Wp.rearrange("(m p) k -> p m k", p=P)[:, 2 * mm : 2 * mm + 2, :]

        chunk_src = [
            tokens(h_ret, 0), hidden(Wr, 0), tokens(h_ret, 1), hidden(Wr, 1),
            tokens(h_prime, 0), hidden(Wc, 0), tokens(h_prime, 1), hidden(Wc, 1),
            channels(0), channels(1), channels(2), channels(3),
        ]
        raws = {}
        groupeds = {}

        def load_chunk(i, in_halves=False):
            raw = raw_pool.tile([P, CHUNK], BF16)
            src = chunk_src[i]
            rows = src.shape[1]
            view = raw[:].rearrange("p (a x) -> p a x", a=rows)
            if in_halves:
                for pair in range(2):
                    part = slice(rows // 2 * pair, rows // 2 * (pair + 1))
                    nc.sync.dma_start(out=view[:, part, :], in_=src[:, part, :])
            else:
                nc.sync.dma_start(out=view, in_=src)
            raws[i] = raw

        rows16 = const.tile([32, P], BF16)
        for v, vec in enumerate((bp, prelu_w, gn_w, gn_b)):
            nc.scalar.dma_start(
                out=rows16[8 * v : 8 * v + 8, :], in_=vec.rearrange("(m i) -> m i", i=P)
            )
        rows32 = const.tile([P, P], F32)
        nc.vector.memset(rows32[:], 0.0)
        nc.scalar.dma_start(
            out=rows32[32:36, :], in_=br.rearrange("(r w) -> r w", w=2 * P).bitcast(F32)
        )
        nc.scalar.dma_start(
            out=rows32[36:40, :], in_=bc.rearrange("(r w) -> r w", w=2 * P).bitcast(F32)
        )
        for n, i in enumerate(CHUNK_ORDER[:RAW_BUFS]):
            load_chunk(i, in_halves=(n < HALVED))

        warm = const.tile([P, 1], F32)
        nc.vector.memset(warm[:], 0.0)
        nc.scalar.activation(out=warm[:], in_=warm[:], func=ACT.Gelu)

        ident = const.tile([P, P], F32)
        masks.make_identity(nc, ident[:])
        group_mean = const.tile([P, P], F32)
        nc.vector.memset(group_mean[:], 0.0)
        nc.vector.memset(group_mean[0:64, 0:64], 1.0 / GROUP_SIZE)
        nc.vector.memset(group_mean[64:128, 64:128], 1.0 / GROUP_SIZE)
        neg_half = const.tile([P, 1], F32)
        nc.vector.memset(neg_half[:], -0.5)
        sums = const.tile([P, N_TILES, 16], F32)
        nc.vector.memset(sums[:], 0.0)

        chan = const.tile([P, 32], F32)
        bias_words = const.tile([P, 8], F32)
        bias1 = const.tile([P, 16], F32)
        neg_bp = const.tile([P, N_TILES], F32)
        one_minus_w = const.tile([P, N_TILES], F32)
        turned_of = {}

        def turn_vectors():
            turned = psum.tile([P, 4, P], F32, tag="tp")
            nc.tensor.transpose(turned[:, 0, :], rows32[:], ident[:])
            turned_of[0] = turned

        def spread_vectors():
            turned = turned_of[0]
            nc.vector.tensor_copy(out=bias_words[:], in_=turned[:, 0, 32:40])
            nc.vector.tensor_copy(out=chan[:], in_=turned[:, 0, 0:32])
            nc.vector.tensor_copy(out=bias1[:], in_=bias_words[:].bitcast(BF16))
            nc.vector.tensor_scalar_mul(out=neg_bp[:], in0=chan[:, 0:8], scalar1=-1.0)
            nc.vector.tensor_scalar(
                out=one_minus_w[:], in0=chan[:, 8:16], scalar1=-1.0, scalar2=1.0,
                op0=ALU.mult, op1=ALU.add,
            )
            nc.vector.tensor_scalar_mul(out=sums[:, :, 7], in0=chan[:, 0:8], scalar1=float(ROWS))

        codes_in = const.tile([P, N_CHUNKS, CHUNK_WORDS], U32, align_bytes=64)
        scales_in = const.tile([P, N_CHUNKS, CHUNK_WORDS], U8, align_bytes=64)
        codes_ac = const.tile([P, N_UNITS, HALF], U32, align_bytes=64)
        scales_ac = const.tile([P, N_UNITS, HALF], U8, align_bytes=64)

        def transpose_chunk(i, vector_banks):
            words = raws[i][:].bitcast(F32).rearrange("p (b w) -> p b w", b=4)
            grouped = grouped_pool.tile([P, CHUNK], BF16, align_bytes=64)
            grouped_words = grouped[:].bitcast(F32).rearrange("p (g c u) -> p g c u", g=2, u=2)
            for pair in range(2):
                for g in range(2):
                    bank = psum.tile([P, 2, 2 * P], F32, tag="tp")
                    for u in range(2):
                        for s in range(2):
                            nc.tensor.transpose(
                                bank[:, u, P * s : P * (s + 1)],
                                words[:, 2 * pair + s, 256 * g + P * u : 256 * g + P * (u + 1)],
                                ident[:],
                            )
                    dst = grouped_words[:, g, 2 * P * pair : 2 * P * (pair + 1), :]
                    src = bank[:].rearrange("p u c -> p c u")
                    if 2 * pair + g in vector_banks:
                        nc.vector.tensor_copy(out=dst, in_=src)
                    else:
                        nc.scalar.copy(out=dst, in_=src)
            groupeds[i] = grouped

        def quantise_chunk(i):
            nc.vector.quantize_mx(
                out=codes_in[:, i, :].bitcast(FP8X4), scales=scales_in[:, i, :], in_=groupeds[i][:]
            )

        planes_of = {}
        regrouped_of = {}

        def operands(k):
            s, jj, half = k // 4, (k // 2) % 2, k % 2
            return 4 * s + 2 * half, 4 * s + 2 * jj + 1, 8 * s + 4 * jj

        def stage1_gelu(k):
            h_chunk, w_chunk, col = operands(k)
            planes = stage1.tile([P, 4, HALF], BF16)
            for t in range(4):
                acc = psum.tile([P, HALF], F32, tag="mx")
                for g in range(2):
                    w_cols = slice(HALF * g + P * t, HALF * g + P * (t + 1))
                    h_cols = slice(HALF * g, HALF * (g + 1))
                    nc.tensor.matmul_mx(
                        out=acc[:],
                        lhsT=codes_in[:, w_chunk, w_cols].bitcast(FP8X4),
                        lhsT_scale=scales_in[:, w_chunk, w_cols],
                        rhs=codes_in[:, h_chunk, h_cols].bitcast(FP8X4),
                        rhs_scale=scales_in[:, h_chunk, h_cols],
                        start=(g == 0),
                        stop=(g == 1),
                    )
                nc.scalar.activation(
                    out=planes[:, t, :], in_=acc[:], func=ACT.Gelu,
                    bias=bias1[:, col + t : col + t + 1], scale=1.0,
                )
            planes_of[k] = planes

        def regroup(k):
            regrouped = stage1.tile([P, HALF, 4], BF16, align_bytes=64)
            nc.vector.tensor_copy(
                out=regrouped[:].rearrange("p (c i) t -> p c t i", i=4),
                in_=planes_of[k][:].rearrange("p t (c i) -> p c t i", i=4),
            )
            regrouped_of[k] = regrouped

        def stage1_linear(k, unit_between, chunk_between):
            h_chunk, w_chunk, col = operands(k)
            regrouped = stage1.tile([P, HALF, 4], BF16, align_bytes=64)
            for b in range(4):
                if b == 1:
                    quantise_unit(unit_between)
                if b == 2 and chunk_between is not None:
                    quantise_chunk(chunk_between)
                acc = psum.tile([P, 4, P], F32, tag="mx")
                for t in range(4):
                    for g in range(2):
                        w_cols = slice(HALF * g + P * t, HALF * g + P * (t + 1))
                        h_cols = slice(HALF * g + P * b, HALF * g + P * (b + 1))
                        nc.tensor.matmul_mx(
                            out=acc[:, t, :],
                            lhsT=codes_in[:, w_chunk, w_cols].bitcast(FP8X4),
                            lhsT_scale=scales_in[:, w_chunk, w_cols],
                            rhs=codes_in[:, h_chunk, h_cols].bitcast(FP8X4),
                            rhs_scale=scales_in[:, h_chunk, h_cols],
                            start=(g == 0),
                            stop=(g == 1),
                        )
                nc.vector.tensor_tensor(
                    out=regrouped[:, P * b : P * (b + 1), :],
                    in0=acc[:].rearrange("p t n -> p n t"),
                    in1=bias1[:, col : col + 4].unsqueeze(1).to_broadcast([P, P, 4]),
                    op=ALU.add,
                )
            regrouped_of[k] = regrouped

        def quantise_unit(k):
            nc.vector.quantize_mx(
                out=codes_ac[:, k, :].bitcast(FP8X4), scales=scales_ac[:, k, :],
                in_=regrouped_of[k][:].rearrange("p n t -> p (n t)"),
            )

        shifted_of = {}
        acc_of = {}
        wide_of = {}
        staged_of = {}
        norm_of = {}
        normed_of = {}

        def pieces_of(m):
            return LAST_PIECES if m == N_TILES - 1 else 2

        def stage2_piece(m, j):
            w_chunk, m2 = 8 + m // 2, m % 2
            width = ROWS // pieces_of(m)
            half, inside = (width * j) // HALF, (width * j) % HALF
            if j == 0:
                shifted = stage2.tile([P, ROWS], F32, bufs=N_TILES)
                shifted_of[m] = shifted
            acc = psum.tile([P, HALF], F32, tag="mx")
            for g in range(4):
                w0 = HALF * (g % 2) + P * (2 * m2 + g // 2)
                nc.tensor.matmul_mx(
                    out=acc[:, 0:width],
                    lhsT=codes_in[:, w_chunk, w0 : w0 + P].bitcast(FP8X4),
                    lhsT_scale=scales_in[:, w_chunk, w0 : w0 + P],
                    rhs=codes_ac[:, 2 * g + half, inside : inside + width].bitcast(FP8X4),
                    rhs_scale=scales_ac[:, 2 * g + half, inside : inside + width],
                    start=(g == 0),
                    stop=(g == 3),
                )
            acc_of[(m, j)] = acc

        def prelu_piece(m, j):
            width = ROWS // pieces_of(m)
            acc = acc_of[(m, j)]
            neg_part = stage2.tile([P, HALF], F32)
            nc.scalar.activation(
                out=neg_part[:, 0:width], in_=acc[:, 0:width], func=ACT.Relu, bias=neg_bp[:, m : m + 1], scale=-1.0
            )
            nc.vector.scalar_tensor_tensor(
                out=shifted_of[m][:, width * j : width * (j + 1)], in0=neg_part[:, 0:width],
                scalar=one_minus_w[:, m : m + 1], in1=acc[:, 0:width], op0=ALU.mult, op1=ALU.add,
                accum_out=sums[:, m, j : j + 1],
            )

        def square_piece(m, j):
            width = ROWS // pieces_of(m)
            squares = stage2.tile([P, HALF], BF16)
            nc.scalar.activation(
                out=squares[:, 0:width], in_=shifted_of[m][:, width * j : width * (j + 1)], func=ACT.Square,
                bias=chan[:, m : m + 1], scale=1.0, accum_out=sums[:, m, 8 + j : 9 + j],
            )

        def square_sums(m):
            for j in range(pieces_of(m)):
                square_piece(m, j)

        def statistics(m):
            spread = psum.tile([P, 4, P], F32, tag="tp")
            nc.tensor.matmul(
                out=spread[:, 0, 0:16], lhsT=group_mean[:], rhs=sums[:, m, :], start=True, stop=True
            )
            moments = small.tile([P, 2], F32)
            nc.vector.tensor_reduce(
                out=moments[:], in_=spread[:, 0, 0:16].rearrange("p (b c) -> p b c", b=2),
                axis=mybir.AxisListType.X, op=ALU.add,
            )
            norm = small.tile([P, 8], F32)
            mean = moments[:, 0:1]
            nc.gpsimd.tensor_tensor(out=norm[:, 0:1], in0=mean, in1=mean, op=ALU.mult)
            nc.gpsimd.tensor_scalar(
                out=norm[:, 1:2], in0=moments[:, 1:2], scalar1=norm[:, 0:1], scalar2=EPS,
                op0=ALU.subtract, op1=ALU.add,
            )
            nc.gpsimd.tensor_tensor(out=norm[:, 2:3], in0=norm[:, 1:2], in1=neg_half[:], op=ALU.pow)
            nc.gpsimd.tensor_tensor(
                out=norm[:, 3:4], in0=norm[:, 2:3], in1=chan[:, 16 + m : 17 + m], op=ALU.mult
            )
            nc.gpsimd.tensor_tensor(
                out=norm[:, 4:5], in0=chan[:, m : m + 1], in1=mean, op=ALU.subtract
            )
            nc.gpsimd.tensor_scalar(
                out=norm[:, 5:6], in0=norm[:, 4:5], scalar1=norm[:, 3:4],
                scalar2=chan[:, 24 + m : 25 + m], op0=ALU.mult, op1=ALU.add,
            )
            norm_of[m] = norm

        def normalise_piece(m, j, pieces):
            width = ROWS // pieces
            part = shifted_of[m][:, width * j : width * (j + 1)]
            nc.vector.tensor_scalar(
                out=part, in0=part, scalar1=norm_of[m][:, 3:4], scalar2=norm_of[m][:, 5:6],
                op0=ALU.mult, op1=ALU.add,
            )

        def normalise(m):
            normalise_piece(m, 0, 1)

        def turn_back(m, j, pieces, engine):
            if j == 0:
                staged = stage2.tile([P, 8, P], F32, bufs=2)
                staged_of[m] = staged
            staged = staged_of[m]
            n = 8 // pieces
            bank = psum.tile([P, 4, P], F32, tag="tp")
            for r in range(n):
                c0 = P * (n * j + r)
                nc.tensor.transpose(bank[:, r, :], shifted_of[m][:, c0 : c0 + P], ident[:])
            if engine == "scalar":
                nc.scalar.copy(out=staged[:, n * j : n * (j + 1), :], in_=bank[:, 0:n, :])
            else:
                nc.vector.tensor_copy(out=staged[:, n * j : n * (j + 1), :], in_=bank[:, 0:n, :])

        def store(m, rows):
            dst = out.rearrange("(p r) c -> p r c", r=8)[:, :, P * m : P * (m + 1)]
            nc.sync.dma_start(out=dst[:, rows, :], in_=staged_of[m][:, rows, :])

        def store_tile(m):
            for half in range(2):
                turn_back(m, half, 2, "scalar" if half == 0 else "vector")
            store(m, slice(0, 8))

        def pair_tile(q, t):
            if t == 0:
                wide_of[q] = [
                    stage2.tile([P, 4, 2 * P], F32, name="wide%d" % half, bufs=2) for half in range(2)
                ]
            m = 2 * q + t
            for half in range(2):
                bank = psum.tile([P, 4, P], F32, tag="tp")
                for r in range(4):
                    c0 = HALF * half + P * r
                    nc.tensor.transpose(bank[:, r, :], shifted_of[m][:, c0 : c0 + P], ident[:])
                dst = wide_of[q][half][:, :, P * t : P * (t + 1)]
                if half == 0:
                    nc.scalar.copy(out=dst, in_=bank[:])
                else:
                    nc.vector.tensor_copy(out=dst, in_=bank[:])

        def pair_store(q):
            dst = out.rearrange("(p r) c -> p r c", r=8)[:, :, 2 * P * q : 2 * P * (q + 1)]
            for half in range(2):
                nc.sync.dma_start(out=dst[:, 4 * half : 4 * half + 4, :], in_=wide_of[q][half][:])

        def finish_last(m, pieces):
            n = 8 // pieces
            for j in range(pieces):
                normalise_piece(m, j, pieces)
            for j in range(pieces):
                turn_back(m, j, pieces, "scalar" if j % 2 == 0 else "vector")
                store(m, slice(n * j, n * (j + 1)))

        transpose_chunk(0, (0, 2))
        transpose_chunk(1, (0, 2))
        quantise_chunk(0)
        nc.vector.tensor_copy(out=rows32[0:32, :], in_=rows16[:])
        transpose_chunk(4, ())
        turn_vectors()
        quantise_chunk(1)
        spread_vectors()
        transpose_chunk(5, ())
        quantise_chunk(4)
        for j, k in enumerate(UNIT_ORDER):
            before = CHUNK_ORDER[j + LEAD - 1] if j + LEAD - 1 < FIRST_LATE else None
            if k < 4:
                if before is not None:
                    quantise_chunk(before)
                if j > 0:
                    quantise_unit(UNIT_ORDER[j - 1])
                stage1_gelu(k)
            else:
                stage1_linear(k, UNIT_ORDER[j - 1], before)
            transpose_chunk(CHUNK_ORDER[j + LEAD], ())
            if j + RAW_BUFS < N_CHUNKS:
                load_chunk(CHUNK_ORDER[j + RAW_BUFS])
            if k < 4:
                regroup(k)
        quantise_unit(UNIT_ORDER[-1])

        for step in range(N_TILES):
            for j in range(pieces_of(step)):
                stage2_piece(step, j)
                if j == pieces_of(step) - 1 and step > 0:
                    statistics(step - 1)
                prelu_piece(step, j)
            if step in LATE_STEPS:
                quantise_chunk(FIRST_LATE + LATE_STEPS.index(step))
            if step == N_TILES - 1:
                square_sums(step)
            if step >= 2:
                normalise(step - 2)
            if step in (4, 6):
                pair_tile(step // 2 - 2, 0)
                pair_tile(step // 2 - 2, 1)
                pair_store(step // 2 - 2)
            if step < N_TILES - 1:
                square_sums(step)
        pair_tile(2, 0)
        statistics(7)
        normalise(6)
        pair_tile(2, 1)
        pair_store(2)
        store_tile(6)
        finish_last(7, 4)
